import numpy as np
import ml_dtypes

BF16 = ml_dtypes.bfloat16


def bf(x):
    return np.asarray(x, np.float32).astype(BF16)


def f32(x):
    return np.asarray(x, np.float32)


def f64(x):
    return np.asarray(x).astype(np.float64)


def striped(idx):
    return np.tile(idx.reshape(-1, 16).T, (8, 1))


C, D, S, H, K, N = 256, 384, 1024, 512, 8, 4096
EPS = 1e-5
SC = 0.05


def sigmoid(v):
    return 1.0 / (1.0 + np.exp(-v))


def normed(z):
    z = z - z.mean(axis=0, keepdims=True)
    return z * np.sqrt((1.0 - EPS) / (z * z).mean(axis=0, keepdims=True))


def setup_inputs():
    return {"cond": f32(normed(np.random.standard_normal((D, S)))), "cond_w": f32(1.0 + 0.1 * np.random.standard_normal((D, 1))), "w_ada": bf(SC * np.random.standard_normal((D, C))), "b_ada": f32(0.1 * np.random.standard_normal((C, 1))), "hn": f32(normed(np.random.standard_normal((C, N)))), "offs": striped(np.concatenate([np.random.permutation(S)[:H] for _ in range(K)]))}


def reference(cond, cond_w, w_ada, b_ada, hn, offs):
    idx = offs[:16].T.reshape(-1)
    ada = sigmoid(f64(w_ada).T @ (f64(cond) * f64(cond_w)) + f64(b_ada))
    return ada[:, idx] * f64(hn)

@@ -1,0 +1,79 @@
+import concourse.mybir as mybir
+
+F32 = mybir.dt.float32
+BF16 = mybir.dt.bfloat16
+U16 = mybir.dt.uint16
+MULT = mybir.AluOpType.mult
+SIGMOID = mybir.ActivationFunctionType.Sigmoid
+
+P = 128
+FEATURES = 384
+RESIDUES = 1024
+CHANNELS = 256
+FRAMES = 4096
+K_BLOCKS = FEATURES // P
+C_BLOCKS = CHANNELS // P
+BANK = 512
+HALVES = RESIDUES // BANK
+PIECE = 512
+PIECES = FRAMES // PIECE
+
+FLOPS = 2 * FEATURES * CHANNELS * RESIDUES
+
+
+def tile_blocktransformerpairbias_kernel(tc, cond, cond_w, w_ada, b_ada, hn, offs, out):
+    nc = tc.nc
+    cond_v = cond.rearrange("(p k) r -> p k r", k=K_BLOCKS)
+    gain_v = cond_w.rearrange("(p k) o -> p (k o)", k=K_BLOCKS)
+    w_v = w_ada.rearrange("(p k) c -> p k c", k=K_BLOCKS)
+
+    with (
+        tc.tile_pool(name="held", bufs=1) as held,
+        tc.tile_pool(name="frames", bufs=C_BLOCKS * PIECES) as frames,
+        tc.psum_pool(name="psum", bufs=C_BLOCKS * HALVES) as psum,
+    ):
+        offsets = held.tile([P, FRAMES // 16], U16, name="offsets")
+        gain = held.tile([P, K_BLOCKS], F32, name="gain")
+        weights = held.tile([P, K_BLOCKS, CHANNELS], BF16, name="weights")
+        cond_f32 = held.tile([P, K_BLOCKS, RESIDUES], F32, name="cond_f32")
+        cond_bf16 = held.tile([P, K_BLOCKS, RESIDUES], BF16, name="cond_bf16")
+        bias = [held.tile([P, 1], F32, name=f"bias{b}") for b in range(C_BLOCKS)]
+        ada = [held.tile([P, RESIDUES], F32, name=f"ada{b}") for b in range(C_BLOCKS)]
+
+        nc.scalar.dma_start(gain[:], gain_v)
+        nc.gpsimd.dma_start(weights[:], w_v)
+        for b in range(C_BLOCKS):
+            nc.gpsimd.dma_start(bias[b][:], b_ada[b * P : (b + 1) * P, :])
+        for h in range(HALVES):
+            cols = slice(h * BANK, (h + 1) * BANK)
+            for k in range(K_BLOCKS):
+                queue = nc.sync if (h * K_BLOCKS + k) % 2 == 0 else nc.scalar
+                queue.dma_start(cond_f32[:, k, cols], cond_v[:, k, cols])
+        nc.sync.dma_start(offsets[:], offs)
+
+        for h in range(HALVES):
+            cols = slice(h * BANK, (h + 1) * BANK)
+            for k in range(K_BLOCKS):
+                nc.vector.tensor_scalar_mul(cond_bf16[:, k, cols], cond_f32[:, k, cols], gain[:, k : k + 1])
+            for b in range(C_BLOCKS):
+                acc = psum.tile([P, BANK], F32, name="acc")
+                for k in range(K_BLOCKS):
+                    nc.tensor.matmul(
+                        acc[:],
+                        weights[:, k, b * P : (b + 1) * P],
+                        cond_bf16[:, k, cols],
+                        start=(k == 0),
+                        stop=(k == K_BLOCKS - 1),
+                    )
+                nc.scalar.activation(ada[b][:, cols], acc[:], SIGMOID, bias=bias[b][:, 0:1], scale=1.0)
+
+        for b in range(C_BLOCKS):
+            rows = slice(b * P, (b + 1) * P)
+            for i in range(PIECES):
+                cols = slice(i * PIECE, (i + 1) * PIECE)
+                hn_piece = frames.tile([P, PIECE], F32, name="hn_piece")
+                nc.sync.dma_start(hn_piece[:], hn[rows, cols])
+                product = frames.tile([P, PIECE], F32, name="product")
+                picked = ada[b][:].indirect(offsets[:, i * (PIECE // 16) : (i + 1) * (PIECE // 16)])
+                nc.vector.tensor_tensor(product[:], picked, hn_piece[:], MULT)
+                nc.scalar.dma_start(out[rows, cols], product[:])

@@ -41,15 +41,19 @@ def tile_blocktransformerpairbias_kernel(tc, cond, cond_w, w_ada, b_ada, hn, off
         ada = [held.tile([P, RESIDUES], F32, name=f"ada{b}") for b in range(C_BLOCKS)]
 
         nc.scalar.dma_start(gain[:], gain_v)
-        nc.gpsimd.dma_start(weights[:], w_v)
-        for b in range(C_BLOCKS):
-            nc.gpsimd.dma_start(bias[b][:], b_ada[b * P : (b + 1) * P, :])
+        nc.sync.dma_start(weights[:], w_v)
         for h in range(HALVES):
             cols = slice(h * BANK, (h + 1) * BANK)
             for k in range(K_BLOCKS):
-                queue = nc.sync if (h * K_BLOCKS + k) % 2 == 0 else nc.scalar
+                queue = nc.scalar if (h * K_BLOCKS + k) % 2 == 0 else nc.sync
                 queue.dma_start(cond_f32[:, k, cols], cond_v[:, k, cols])
+        for b in range(C_BLOCKS):
+            nc.scalar.dma_start(bias[b][:], b_ada[b * P : (b + 1) * P, :])
         nc.sync.dma_start(offsets[:], offs)
+
+        scratch = held.tile([P, 1], F32, name="scratch")
+        nc.vector.memset(scratch[:], 0.0)
+        nc.scalar.activation(scratch[:], scratch[:], SIGMOID)
 
         for h in range(HALVES):
             cols = slice(h * BANK, (h + 1) * BANK)

@@ -15,7 +15,7 @@ K_BLOCKS = FEATURES // P
 C_BLOCKS = CHANNELS // P
 BANK = 512
 HALVES = RESIDUES // BANK
-PIECE = 512
+PIECE = 1024
 PIECES = FRAMES // PIECE
 
 FLOPS = 2 * FEATURES * CHANNELS * RESIDUES

@@ -59,7 +59,10 @@ def tile_blocktransformerpairbias_kernel(tc, cond, cond_w, w_ada, b_ada, hn, off
             cols = slice(h * BANK, (h + 1) * BANK)
             for k in range(K_BLOCKS):
                 nc.vector.tensor_scalar_mul(cond_bf16[:, k, cols], cond_f32[:, k, cols], gain[:, k : k + 1])
-            for b in range(C_BLOCKS):
+
+        for b in range(C_BLOCKS):
+            for h in range(HALVES):
+                cols = slice(h * BANK, (h + 1) * BANK)
                 acc = psum.tile([P, BANK], F32, name="acc")
                 for k in range(K_BLOCKS):
                     nc.tensor.matmul(

@@ -29,7 +29,7 @@ def tile_blocktransformerpairbias_kernel(tc, cond, cond_w, w_ada, b_ada, hn, off
 
     with (
         tc.tile_pool(name="held", bufs=1) as held,
-        tc.tile_pool(name="frames", bufs=C_BLOCKS * PIECES) as frames,
+        tc.tile_pool(name="frames", bufs=C_BLOCKS * PIECES + 2) as frames,
         tc.psum_pool(name="psum", bufs=C_BLOCKS * HALVES) as psum,
     ):
         offsets = held.tile([P, FRAMES // 16], U16, name="offsets")
@@ -76,11 +76,16 @@ def tile_blocktransformerpairbias_kernel(tc, cond, cond_w, w_ada, b_ada, hn, off
 
         for b in range(C_BLOCKS):
             rows = slice(b * P, (b + 1) * P)
-            for i in range(PIECES):
-                cols = slice(i * PIECE, (i + 1) * PIECE)
-                hn_piece = frames.tile([P, PIECE], F32, name="hn_piece")
+            widths = [PIECE] * PIECES
+            if b == C_BLOCKS - 1:
+                widths[-1:] = [PIECE // 2, PIECE // 4, PIECE // 4]
+            start = 0
+            for width in widths:
+                cols = slice(start, start + width)
+                hn_piece = frames.tile([P, width], F32, name="hn_piece")
                 nc.sync.dma_start(hn_piece[:], hn[rows, cols])
-                product = frames.tile([P, PIECE], F32, name="product")
-                picked = ada[b][:].indirect(offsets[:, i * (PIECE // 16) : (i + 1) * (PIECE // 16)])
+                product = frames.tile([P, width], F32, name="product")
+                picked = ada[b][:].indirect(offsets[:, start // 16 : (start + width) // 16])
                 nc.vector.tensor_tensor(product[:], picked, hn_piece[:], MULT)
                 nc.scalar.dma_start(out[rows, cols], product[:])
+                start += width

@@ -30,7 +30,7 @@ def tile_blocktransformerpairbias_kernel(tc, cond, cond_w, w_ada, b_ada, hn, off
     with (
         tc.tile_pool(name="held", bufs=1) as held,
         tc.tile_pool(name="frames", bufs=C_BLOCKS * PIECES + 2) as frames,
-        tc.psum_pool(name="psum", bufs=C_BLOCKS * HALVES) as psum,
+        tc.psum_pool(name="psum", bufs=HALVES) as psum,
     ):
         offsets = held.tile([P, FRAMES // 16], U16, name="offsets")
         gain = held.tile([P, K_BLOCKS], F32, name="gain")

@@ -15,6 +15,7 @@ K_BLOCKS = FEATURES // P
 C_BLOCKS = CHANNELS // P
 BANK = 512
 HALVES = RESIDUES // BANK
+GROUPS = [slice(0, BANK), slice(BANK, BANK + BANK // 2), slice(BANK + BANK // 2, RESIDUES)]
 PIECE = 1024
 PIECES = FRAMES // PIECE
 
@@ -30,7 +31,7 @@ def tile_blocktransformerpairbias_kernel(tc, cond, cond_w, w_ada, b_ada, hn, off
     with (
         tc.tile_pool(name="held", bufs=1) as held,
         tc.tile_pool(name="frames", bufs=C_BLOCKS * PIECES + 2) as frames,
-        tc.psum_pool(name="psum", bufs=HALVES) as psum,
+        tc.psum_pool(name="psum", bufs=len(GROUPS)) as psum,
     ):
         offsets = held.tile([P, FRAMES // 16], U16, name="offsets")
         gain = held.tile([P, K_BLOCKS], F32, name="gain")
@@ -55,24 +56,24 @@ def tile_blocktransformerpairbias_kernel(tc, cond, cond_w, w_ada, b_ada, hn, off
         nc.vector.memset(scratch[:], 0.0)
         nc.scalar.activation(scratch[:], scratch[:], SIGMOID)
 
-        for h in range(HALVES):
-            cols = slice(h * BANK, (h + 1) * BANK)
+        for groups in (GROUPS[:1], GROUPS[1:]):
             for k in range(K_BLOCKS):
-                nc.vector.tensor_scalar_mul(cond_bf16[:, k, cols], cond_f32[:, k, cols], gain[:, k : k + 1])
+                for cols in groups:
+                    nc.vector.tensor_scalar_mul(cond_bf16[:, k, cols], cond_f32[:, k, cols], gain[:, k : k + 1])
 
         for b in range(C_BLOCKS):
-            for h in range(HALVES):
-                cols = slice(h * BANK, (h + 1) * BANK)
+            for cols in GROUPS:
+                width = cols.stop - cols.start
                 acc = psum.tile([P, BANK], F32, name="acc")
                 for k in range(K_BLOCKS):
                     nc.tensor.matmul(
-                        acc[:],
+                        acc[:, :width],
                         weights[:, k, b * P : (b + 1) * P],
                         cond_bf16[:, k, cols],
                         start=(k == 0),
                         stop=(k == K_BLOCKS - 1),
                     )
-                nc.scalar.activation(ada[b][:, cols], acc[:], SIGMOID, bias=bias[b][:, 0:1], scale=1.0)
+                nc.scalar.activation(ada[b][:, cols], acc[:, :width], SIGMOID, bias=bias[b][:, 0:1], scale=1.0)
 
         for b in range(C_BLOCKS):
             rows = slice(b * P, (b + 1) * P)

@@ -14,8 +14,12 @@ FRAMES = 4096
 K_BLOCKS = FEATURES // P
 C_BLOCKS = CHANNELS // P
 BANK = 512
-HALVES = RESIDUES // BANK
 GROUPS = [slice(0, BANK), slice(BANK, BANK + BANK // 2), slice(BANK + BANK // 2, RESIDUES)]
+CHUNKS = (
+    [(k, slice(0, BANK)) for k in range(K_BLOCKS)]
+    + [(k, slice(BANK, RESIDUES)) for k in range(K_BLOCKS - 1)]
+    + [(K_BLOCKS - 1, cols) for cols in GROUPS[1:]]
+)
 PIECE = 1024
 PIECES = FRAMES // PIECE
 
@@ -27,6 +31,7 @@ def tile_blocktransformerpairbias_kernel(tc, cond, cond_w, w_ada, b_ada, hn, off
     cond_v = cond.rearrange("(p k) r -> p k r", k=K_BLOCKS)
     gain_v = cond_w.rearrange("(p k) o -> p (k o)", k=K_BLOCKS)
     w_v = w_ada.rearrange("(p k) c -> p k c", k=K_BLOCKS)
+    bias_v = b_ada.rearrange("(b p) o -> p (b o)", p=P)
 
     with (
         tc.tile_pool(name="held", bufs=1) as held,
@@ -38,18 +43,15 @@ def tile_blocktransformerpairbias_kernel(tc, cond, cond_w, w_ada, b_ada, hn, off
         weights = held.tile([P, K_BLOCKS, CHANNELS], BF16, name="weights")
         cond_f32 = held.tile([P, K_BLOCKS, RESIDUES], F32, name="cond_f32")
         cond_bf16 = held.tile([P, K_BLOCKS, RESIDUES], BF16, name="cond_bf16")
-        bias = [held.tile([P, 1], F32, name=f"bias{b}") for b in range(C_BLOCKS)]
+        bias = held.tile([P, C_BLOCKS], F32, name="bias")
         ada = [held.tile([P, RESIDUES], F32, name=f"ada{b}") for b in range(C_BLOCKS)]
 
         nc.scalar.dma_start(gain[:], gain_v)
         nc.sync.dma_start(weights[:], w_v)
-        for h in range(HALVES):
-            cols = slice(h * BANK, (h + 1) * BANK)
-            for k in range(K_BLOCKS):
-                queue = nc.scalar if (h * K_BLOCKS + k) % 2 == 0 else nc.sync
-                queue.dma_start(cond_f32[:, k, cols], cond_v[:, k, cols])
-        for b in range(C_BLOCKS):
-            nc.scalar.dma_start(bias[b][:], b_ada[b * P : (b + 1) * P, :])
+        for i, (k, cols) in enumerate(CHUNKS):
+            queue = nc.scalar if i % 2 == 0 else nc.sync
+            queue.dma_start(cond_f32[:, k, cols], cond_v[:, k, cols])
+        nc.sync.dma_start(bias[:], bias_v)
         nc.sync.dma_start(offsets[:], offs)
 
         scratch = held.tile([P, 1], F32, name="scratch")
@@ -73,7 +75,7 @@ def tile_blocktransformerpairbias_kernel(tc, cond, cond_w, w_ada, b_ada, hn, off
                         start=(k == 0),
                         stop=(k == K_BLOCKS - 1),
                     )
-                nc.scalar.activation(ada[b][:, cols], acc[:, :width], SIGMOID, bias=bias[b][:, 0:1], scale=1.0)
+                nc.scalar.activation(ada[b][:, cols], acc[:, :width], SIGMOID, bias=bias[:, b : b + 1], scale=1.0)
 
         for b in range(C_BLOCKS):
             rows = slice(b * P, (b + 1) * P)

@@ -47,10 +47,11 @@ def tile_blocktransformerpairbias_kernel(tc, cond, cond_w, w_ada, b_ada, hn, off
         ada = [held.tile([P, RESIDUES], F32, name=f"ada{b}") for b in range(C_BLOCKS)]
 
         nc.scalar.dma_start(gain[:], gain_v)
-        nc.sync.dma_start(weights[:], w_v)
         for i, (k, cols) in enumerate(CHUNKS):
-            queue = nc.scalar if i % 2 == 0 else nc.sync
+            queue = nc.sync if i % 2 == 0 else nc.scalar
             queue.dma_start(cond_f32[:, k, cols], cond_v[:, k, cols])
+            if i == 0:
+                nc.sync.dma_start(weights[:], w_v)
         nc.sync.dma_start(bias[:], bias_v)
         nc.sync.dma_start(offsets[:], offs)
 

@@ -14,11 +14,12 @@ FRAMES = 4096
 K_BLOCKS = FEATURES // P
 C_BLOCKS = CHANNELS // P
 BANK = 512
-GROUPS = [slice(0, BANK), slice(BANK, BANK + BANK // 2), slice(BANK + BANK // 2, RESIDUES)]
+GROUP = BANK // 2
+GROUPS = [slice(start, start + GROUP) for start in range(0, RESIDUES, GROUP)]
 CHUNKS = (
     [(k, slice(0, BANK)) for k in range(K_BLOCKS)]
     + [(k, slice(BANK, RESIDUES)) for k in range(K_BLOCKS - 1)]
-    + [(K_BLOCKS - 1, cols) for cols in GROUPS[1:]]
+    + [(K_BLOCKS - 1, cols) for cols in GROUPS[2:]]
 )
 PIECE = 1024
 PIECES = FRAMES // PIECE
@@ -59,24 +60,23 @@ def tile_blocktransformerpairbias_kernel(tc, cond, cond_w, w_ada, b_ada, hn, off
         nc.vector.memset(scratch[:], 0.0)
         nc.scalar.activation(scratch[:], scratch[:], SIGMOID)
 
-        for groups in (GROUPS[:1], GROUPS[1:]):
+        for groups in (GROUPS[:2], GROUPS[2:]):
             for k in range(K_BLOCKS):
                 for cols in groups:
                     nc.vector.tensor_scalar_mul(cond_bf16[:, k, cols], cond_f32[:, k, cols], gain[:, k : k + 1])
 
         for b in range(C_BLOCKS):
             for cols in GROUPS:
-                width = cols.stop - cols.start
-                acc = psum.tile([P, BANK], F32, name="acc")
+                acc = psum.tile([P, GROUP], F32, name="acc")
                 for k in range(K_BLOCKS):
                     nc.tensor.matmul(
-                        acc[:, :width],
+                        acc[:],
                         weights[:, k, b * P : (b + 1) * P],
                         cond_bf16[:, k, cols],
                         start=(k == 0),
                         stop=(k == K_BLOCKS - 1),
                     )
-                nc.scalar.activation(ada[b][:, cols], acc[:, :width], SIGMOID, bias=bias[:, b : b + 1], scale=1.0)
+                nc.scalar.activation(ada[b][:, cols], acc[:], SIGMOID, bias=bias[:, b : b + 1], scale=1.0)
 
         for b in range(C_BLOCKS):
             rows = slice(b * P, (b + 1) * P)

import concourse.mybir as mybir

F32 = mybir.dt.float32
BF16 = mybir.dt.bfloat16
U16 = mybir.dt.uint16
MULT = mybir.AluOpType.mult
SIGMOID = mybir.ActivationFunctionType.Sigmoid

P = 128
FEATURES = 384
RESIDUES = 1024
CHANNELS = 256
FRAMES = 4096
K_BLOCKS = FEATURES // P
C_BLOCKS = CHANNELS // P
BANK = 512
GROUP = BANK // 2
GROUPS = [slice(start, start + GROUP) for start in range(0, RESIDUES, GROUP)]
CHUNKS = (
    [(k, slice(0, BANK)) for k in range(K_BLOCKS)]
    + [(k, slice(BANK, RESIDUES)) for k in range(K_BLOCKS - 1)]
    + [(K_BLOCKS - 1, cols) for cols in GROUPS[2:]]
)
PIECE = 1024
PIECES = FRAMES // PIECE

FLOPS = 2 * FEATURES * CHANNELS * RESIDUES


def tile_blocktransformerpairbias_kernel(tc, cond, cond_w, w_ada, b_ada, hn, offs, out):
    nc = tc.nc
    cond_v = cond.rearrange("(p k) r -> p k r", k=K_BLOCKS)
    gain_v = cond_w.rearrange("(p k) o -> p (k o)", k=K_BLOCKS)
    w_v = w_ada.rearrange("(p k) c -> p k c", k=K_BLOCKS)
    bias_v = b_ada.rearrange("(b p) o -> p (b o)", p=P)

    with (
        tc.tile_pool(name="held", bufs=1) as held,
        tc.tile_pool(name="frames", bufs=C_BLOCKS * PIECES + 2) as frames,
        tc.psum_pool(name="psum", bufs=len(GROUPS)) as psum,
    ):
        offsets = held.tile([P, FRAMES // 16], U16, name="offsets")
        gain = held.tile([P, K_BLOCKS], F32, name="gain")
        weights = held.tile([P, K_BLOCKS, CHANNELS], BF16, name="weights")
        cond_f32 = held.tile([P, K_BLOCKS, RESIDUES], F32, name="cond_f32")
        cond_bf16 = held.tile([P, K_BLOCKS, RESIDUES], BF16, name="cond_bf16")
        bias = held.tile([P, C_BLOCKS], F32, name="bias")
        ada = [held.tile([P, RESIDUES], F32, name=f"ada{b}") for b in range(C_BLOCKS)]

        nc.scalar.dma_start(gain[:], gain_v)
        for i, (k, cols) in enumerate(CHUNKS):
            queue = nc.sync if i % 2 == 0 else nc.scalar
            queue.dma_start(cond_f32[:, k, cols], cond_v[:, k, cols])
            if i == 0:
                nc.sync.dma_start(weights[:], w_v)
        nc.sync.dma_start(bias[:], bias_v)
        nc.sync.dma_start(offsets[:], offs)

        scratch = held.tile([P, 1], F32, name="scratch")
        nc.vector.memset(scratch[:], 0.0)
        nc.scalar.activation(scratch[:], scratch[:], SIGMOID)

        for groups in (GROUPS[:2], GROUPS[2:]):
            for k in range(K_BLOCKS):
                for cols in groups:
                    nc.vector.tensor_scalar_mul(cond_bf16[:, k, cols], cond_f32[:, k, cols], gain[:, k : k + 1])

        for b in range(C_BLOCKS):
            for cols in GROUPS:
                acc = psum.tile([P, GROUP], F32, name="acc")
                for k in range(K_BLOCKS):
                    nc.tensor.matmul(
                        acc[:],
                        weights[:, k, b * P : (b + 1) * P],
                        cond_bf16[:, k, cols],
                        start=(k == 0),
                        stop=(k == K_BLOCKS - 1),
                    )
                nc.scalar.activation(ada[b][:, cols], acc[:], SIGMOID, bias=bias[:, b : b + 1], scale=1.0)

        for b in range(C_BLOCKS):
            rows = slice(b * P, (b + 1) * P)
            widths = [PIECE] * PIECES
            if b == C_BLOCKS - 1:
                widths[-1:] = [PIECE // 2, PIECE // 4, PIECE // 4]
            start = 0
            for width in widths:
                cols = slice(start, start + width)
                hn_piece = frames.tile([P, width], F32, name="hn_piece")
                nc.sync.dma_start(hn_piece[:], hn[rows, cols])
                product = frames.tile([P, width], F32, name="product")
                picked = ada[b][:].indirect(offsets[:, start // 16 : (start + width) // 16])
                nc.vector.tensor_tensor(product[:], picked, hn_piece[:], MULT)
                nc.scalar.dma_start(out[rows, cols], product[:])
                start += width
